import numpy as np
import ml_dtypes


def mxq(x, axis, fmt="e4m3"):
    dtype, down = {"e4m3": (ml_dtypes.float8_e4m3fn, 7), "e5m2": (ml_dtypes.float8_e5m2, 14)}[fmt]
    v = np.moveaxis(np.asarray(x, np.float32).astype(ml_dtypes.bfloat16).astype(np.float64), axis, -1)
    blocks = v.reshape(v.shape[:-1] + (-1, 32))
    amax = np.abs(blocks).max(-1, keepdims=True)
    byte = np.maximum(np.where(amax > 0, np.frexp(amax)[1] - 1 + 127, 0) - down, 1)
    scale = np.exp2(byte - 127.0)
    codes = (blocks / scale).astype(np.float32).astype(dtype).astype(np.float64)
    return np.moveaxis((codes * scale).reshape(v.shape), -1, axis)


WIDE = False


def mx_kscale(k):
    if not WIDE:
        return np.ones(k)
    levels = np.array([20, -20, 10, -10, 0])
    a = np.random.permutation(np.resize(levels, k // 512 * 4)).reshape(k // 512, 4)
    idx = np.arange(k)
    return np.exp2(a[idx // 512, idx % 128 // 32])


BF16 = ml_dtypes.bfloat16


def bf(x):
    return np.asarray(x, np.float32).astype(BF16)


def f64(x):
    return np.asarray(x).astype(np.float64)


B, S, D, K = 256, 8, 1024, 512


def setup_inputs():
    t = np.exp2(np.round(np.log2(mx_kscale(K)) / 2))
    u = t * t
    q = np.random.standard_normal((B, S, D))
    a = 0.3 * np.random.standard_normal((B, S, 1))
    p = np.random.standard_normal((B, S, D)) + a * q[:, -1:, :]
    W0 = bf(np.random.uniform(0.0, 1.0, (K, D)) * np.sqrt(12.0 / D))
    g = np.random.standard_normal((B, K, S)) * np.exp2(np.random.randint(-12, 1, (B, 1, S))) * 2.0 ** 18 / u[None, :, None]
    p, q = bf(p), bf(q)
    pf, qf, W2 = f64(p), f64(q)[:, -1, :], f64(W0) * f64(W0)
    dot = ((pf * qf[:, None, :]) @ W2.T).transpose(0, 2, 1)
    norm_p = np.sqrt(((pf * pf) @ W2.T).transpose(0, 2, 1))
    norm_q = np.sqrt((qf * qf) @ W2.T)
    return {"p": p, "q": q, "W": bf(f64(W0) * t[:, None]),
            "dot": np.asarray(dot, np.float32), "norm_p": np.asarray(norm_p, np.float32), "norm_q": np.asarray(norm_q, np.float32),
            "grad_out": bf(g.reshape(B, S, K))}


def reference(p, q, W, dot, norm_p, norm_q, grad_out):
    p, q, W = f64(p), f64(q), f64(W)
    dot, norm_p, norm_q = f64(dot), f64(norm_p), f64(norm_q)
    G = f64(grad_out).reshape(B, K, S)
    nq = norm_q[:, :, None]
    ca = -G / (norm_p * nq * D)
    cb = G * dot / (norm_p ** 3 * nq * D)
    ca2 = ca.transpose(0, 2, 1).reshape(B * S, K)
    cb2 = cb.transpose(0, 2, 1).reshape(B * S, K)
    W2 = mxq(W * W, 0, "e4m3")
    m1 = (mxq(ca2, 1, "e5m2") @ W2).reshape(B, S, D)
    m2 = (mxq(cb2, 1, "e5m2") @ W2).reshape(B, S, D)
    return q[:, -1, :][:, None, :] * m1 + p * m2

@@ -1,0 +1,250 @@
+from contextlib import ExitStack
+
+import concourse.mybir as mybir
+from concourse.masks import make_identity
+
+F32 = mybir.dt.float32
+BF16 = mybir.dt.bfloat16
+U32 = mybir.dt.uint32
+U8 = mybir.dt.uint8
+E4M3_X4 = mybir.dt.float8_e4m3fn_x4
+E5M2_X4 = mybir.dt.float8_e5m2_x4
+ACT = mybir.ActivationFunctionType
+ALU = mybir.AluOpType
+
+B, S, D, K = 256, 8, 1024, 512
+P = 128
+PACK = 4
+HALVES = B // P
+CHUNK_K = 128
+CHUNK = CHUNK_K * S
+CHUNKS = K // CHUNK_K
+N_COLS = 512
+LOADS_AHEAD = 2
+P_AHEAD = 3
+
+FLOPS = 2 * 2 * B * S * K * D
+BYTES = 2 * (B * S * D + B * D + K * D + B * S * K) + 4 * (2 * B * K * S + B * K + B * S * D)
+
+
+def tile_mpl_t_v_kernel(tc, p, q, W, dot, norm_p, norm_q, grad_out, out):
+    nc = tc.nc
+    dot_rows = dot.rearrange("b k s -> b (k s)")
+    norm_p_rows = norm_p.rearrange("b k s -> b (k s)")
+    grad_rows = grad_out.rearrange("b s k -> b (s k)")
+
+    with ExitStack() as whole:
+        whole.enter_context(tc.manual_schedule())
+        keep = whole.enter_context(tc.tile_pool(name="keep", bufs=1))
+        grouped_pool = whole.enter_context(tc.tile_pool(name="grouped", bufs=2))
+        p_pool = whole.enter_context(tc.tile_pool(name="p_rows", bufs=P_AHEAD + 1))
+        turned_pool = whole.enter_context(tc.psum_pool(name="turned", bufs=4))
+        product_pool = whole.enter_context(tc.psum_pool(name="product", bufs=2))
+
+        identity = keep.tile([P, P], F32)
+        make_identity(nc, identity[:])
+        w2_codes = keep.tile([P, D], U32, align_bytes=64)
+        w2_scales = keep.tile([P, D], U8, align_bytes=64)
+        halves = range(HALVES)
+        norm_q_sb = [keep.tile([P, K], F32, name="norm_q_sb%d" % h) for h in halves]
+        inv_norm_q = [keep.tile([P, K], F32, name="inv_norm_q%d" % h) for h in halves]
+        q_last = [keep.tile([P, D], BF16, name="q_last%d" % h) for h in halves]
+        ca = [keep.tile([P, K * S], F32, name="ca%d" % h) for h in halves]
+        cb = [keep.tile([P, K * S], F32, name="cb%d" % h) for h in halves]
+        codes = [keep.tile([P, S, 2 * P], U32, name="codes%d" % h, align_bytes=64) for h in halves]
+        scales = [keep.tile([P, S, 2 * P], U8, name="scales%d" % h, align_bytes=64) for h in halves]
+
+        def batch_rows(half):
+            return slice(half * P, (half + 1) * P)
+
+
+        grouped_tiles = {}
+
+        def turn(half, s):
+            grouped = grouped_pool.tile([P, 2, P, PACK], BF16, align_bytes=64)
+            for which, coefficient in enumerate((ca[half], cb[half])):
+                by_k = coefficient[:].rearrange("b (i j s) -> b j s i", j=PACK, s=S)
+                turned = turned_pool.tile([P, PACK, P], F32)
+                for j in range(PACK):
+                    nc.tensor.transpose(turned[:, j, :], by_k[:, j, s, :], identity[:])
+                nc.scalar.copy(out=grouped[:, which], in_=turned[:].rearrange("i j b -> i b j"))
+            grouped_tiles[(half, s)] = grouped
+
+        def quantise(half, s):
+            grouped = grouped_tiles[(half, s)]
+            nc.vector.quantize_mx(
+                out=codes[half][:, s, :].bitcast(E5M2_X4),
+                scales=scales[half][:, s, :],
+                in_=grouped[:].rearrange("i c b j -> i (c b j)"),
+            )
+
+
+        with ExitStack() as coefficient_phase:
+            inputs = coefficient_phase.enter_context(tc.tile_pool(name="inputs", bufs=LOADS_AHEAD + 1))
+            work = coefficient_phase.enter_context(tc.tile_pool(name="work", bufs=2))
+            w_pool = coefficient_phase.enter_context(tc.tile_pool(name="w", bufs=1))
+
+            loaded = {}
+
+            def load_chunk(n):
+                half, c = divmod(n, CHUNKS)
+                cols = slice(c * CHUNK, (c + 1) * CHUNK)
+                norm_p_c = inputs.tile([P, CHUNK], F32)
+                nc.sync.dma_start(out=norm_p_c[:], in_=norm_p_rows[batch_rows(half), cols])
+                grad_c = inputs.tile([P, CHUNK], BF16)
+                nc.sync.dma_start(out=grad_c[:], in_=grad_rows[batch_rows(half), cols])
+                dot_c = inputs.tile([P, CHUNK], F32)
+                nc.sync.dma_start(out=dot_c[:], in_=dot_rows[batch_rows(half), cols])
+                loaded[n] = (norm_p_c, grad_c, dot_c)
+
+            def first_guess(value, factor, width):
+                squared = work.tile([P, width], F32, tag="squared")
+                nc.scalar.activation(out=squared[:], in_=value, func=ACT.Square, scale=factor)
+                guess = work.tile([P, width], F32, tag="guess", bufs=3)
+                nc.scalar.activation(out=guess[:], in_=squared[:], func=ACT.Abs_reciprocal_sqrt)
+                return guess
+
+            def refine(result, value, factor, guess, width):
+                minus_product = work.tile([P, width], F32, tag="minus_product")
+                nc.vector.scalar_tensor_tensor(
+                    out=minus_product[:], in0=value, scalar=-factor, in1=guess[:], op0=ALU.mult, op1=ALU.mult
+                )
+                nc.vector.scalar_tensor_tensor(
+                    out=result, in0=minus_product[:], scalar=2.0, in1=guess[:], op0=ALU.add, op1=ALU.mult
+                )
+
+            def invert_norm_q(half):
+                guess = first_guess(norm_q_sb[half][:], float(D), K)
+                refine(inv_norm_q[half][:], norm_q_sb[half][:], float(D), guess, K)
+
+            guesses = {}
+            inv_squares = {}
+
+            def compute_ca(n):
+                half, c = divmod(n, CHUNKS)
+                norm_p_c, grad_c, dot_c = loaded[n]
+                inv_norm_p = work.tile([P, CHUNK], F32)
+                refine(inv_norm_p[:], norm_p_c[:], 1.0, guesses[n], CHUNK)
+                inv_norm_p_sq = work.tile([P, CHUNK], F32)
+                nc.scalar.activation(out=inv_norm_p_sq[:], in_=inv_norm_p[:], func=ACT.Square)
+                inv_squares[n] = inv_norm_p_sq
+                grad_over_nq = work.tile([P, CHUNK_K, S], F32)
+                nc.vector.tensor_tensor(
+                    out=grad_over_nq[:],
+                    in0=grad_c[:].rearrange("b (k s) -> b k s", s=S),
+                    in1=inv_norm_q[half][:, c * CHUNK_K : (c + 1) * CHUNK_K].unsqueeze(2).to_broadcast([P, CHUNK_K, S]),
+                    op=ALU.mult,
+                )
+                nc.vector.scalar_tensor_tensor(
+                    out=ca[half][:, c * CHUNK : (c + 1) * CHUNK],
+                    in0=grad_over_nq[:].rearrange("b k s -> b (k s)"),
+                    scalar=-1.0,
+                    in1=inv_norm_p[:],
+                    op0=ALU.mult,
+                    op1=ALU.mult,
+                )
+
+            def compute_cb(n):
+                half, c = divmod(n, CHUNKS)
+                norm_p_c, grad_c, dot_c = loaded[n]
+                dot_over_np2 = work.tile([P, CHUNK], F32)
+                nc.vector.tensor_tensor(out=dot_over_np2[:], in0=dot_c[:], in1=inv_squares[n][:], op=ALU.mult)
+                nc.vector.scalar_tensor_tensor(
+                    out=cb[half][:, c * CHUNK : (c + 1) * CHUNK],
+                    in0=ca[half][:, c * CHUNK : (c + 1) * CHUNK],
+                    scalar=-1.0,
+                    in1=dot_over_np2[:],
+                    op0=ALU.mult,
+                    op1=ALU.mult,
+                )
+
+            nc.sync.dma_start(out=norm_q_sb[0][:], in_=norm_q[batch_rows(0), :])
+            for n in range(LOADS_AHEAD):
+                load_chunk(n)
+            nc.sync.dma_start(out=norm_q_sb[1][:], in_=norm_q[batch_rows(1), :])
+            w_rows = w_pool.tile([P, PACK, D], BF16)
+            nc.sync.dma_start(out=w_rows[:], in_=W.rearrange("(i j) d -> i j d", j=PACK))
+            w2_grouped = w_pool.tile([P, D, PACK], BF16, align_bytes=64)
+
+            invert_norm_q(0)
+            guesses[0] = first_guess(loaded[0][0][:], 1.0, CHUNK)
+            for n in range(HALVES * CHUNKS):
+                half, c = divmod(n, CHUNKS)
+                if n + LOADS_AHEAD < HALVES * CHUNKS:
+                    load_chunk(n + LOADS_AHEAD)
+                if n + 1 < HALVES * CHUNKS:
+                    guesses[n + 1] = first_guess(loaded[n + 1][0][:], 1.0, CHUNK)
+                if half == 1:
+                    turn(0, 2 * c)
+                compute_ca(n)
+                if half == 0:
+                    d_cols = slice(c * (D // CHUNKS), (c + 1) * (D // CHUNKS))
+                    nc.scalar.activation(
+                        out=w2_grouped[:, d_cols, :],
+                        in_=w_rows[:, :, d_cols].rearrange("i j d -> i d j"),
+                        func=ACT.Square,
+                    )
+                else:
+                    turn(0, 2 * c + 1)
+                compute_cb(n)
+                if n == 0:
+                    invert_norm_q(1)
+                if half == 1:
+                    quantise(0, 2 * c)
+                    quantise(0, 2 * c + 1)
+            nc.vector.quantize_mx(
+                out=w2_codes[:].bitcast(E4M3_X4),
+                scales=w2_scales[:],
+                in_=w2_grouped[:].rearrange("i d j -> i (d j)"),
+            )
+
+
+        terms = whole.enter_context(tc.tile_pool(name="terms", bufs=4))
+        order = [(half, s) for s in range(S) for half in halves]
+        p_tiles = {}
+
+        def load_p(n):
+            if n < len(order):
+                half, s = order[n]
+                p_tile = p_pool.tile([P, D], BF16)
+                nc.sync.dma_start(out=p_tile[:], in_=p[batch_rows(half), s, :])
+                p_tiles[n] = p_tile
+
+        def write_output(n):
+            half, s = order[n]
+            load_p(n + P_AHEAD)
+            p_tile = p_tiles[n]
+            q_term = terms.tile([P, D], F32)
+            p_term = terms.tile([P, D], F32)
+            for d_cols in (slice(0, N_COLS), slice(N_COLS, D)):
+                m1 = product_pool.tile([P, N_COLS], F32)
+                m2 = product_pool.tile([P, N_COLS], F32)
+                for which, product in enumerate((m1, m2)):
+                    tokens = slice(which * P, (which + 1) * P)
+                    nc.tensor.matmul_mx(
+                        out=product[:],
+                        lhsT=codes[half][:, s, tokens].bitcast(E5M2_X4),
+                        lhsT_scale=scales[half][:, s, tokens],
+                        rhs=w2_codes[:, d_cols].bitcast(E4M3_X4),
+                        rhs_scale=w2_scales[:, d_cols],
+                        start=True,
+                        stop=True,
+                    )
+                nc.vector.tensor_tensor(out=q_term[:, d_cols], in0=m1[:], in1=q_last[half][:, d_cols], op=ALU.mult)
+                nc.vector.tensor_tensor(out=p_term[:, d_cols], in0=m2[:], in1=p_tile[:, d_cols], op=ALU.mult)
+            nc.gpsimd.tensor_tensor(out=q_term[:], in0=q_term[:], in1=p_term[:], op=ALU.add)
+            nc.sync.dma_start(out=out[batch_rows(half), s, :], in_=q_term[:])
+
+        for half in halves:
+            nc.sync.dma_start(out=q_last[half][:], in_=q[batch_rows(half), S - 1, :])
+        for n in range(P_AHEAD):
+            load_p(n)
+        turn(1, 0)
+        quantise(1, 0)
+        for s in range(S):
+            if s + 1 < S:
+                turn(1, s + 1)
+            write_output(2 * s)
+            if s + 1 < S:
+                quantise(1, s + 1)
+            write_output(2 * s + 1)

@@ -20,6 +20,7 @@ CHUNK_K = 128
 CHUNK = CHUNK_K * S
 CHUNKS = K // CHUNK_K
 N_COLS = 512
+ALL_CHUNKS = HALVES * CHUNKS
 LOADS_AHEAD = 2
 P_AHEAD = 3
 
@@ -104,56 +105,76 @@ def tile_mpl_t_v_kernel(tc, p, q, W, dot, norm_p, norm_q, grad_out, out):
                 nc.scalar.activation(out=guess[:], in_=squared[:], func=ACT.Abs_reciprocal_sqrt)
                 return guess
 
-            def refine(result, value, factor, guess, width):
+
+            def newton_product(value, factor, guess, width):
                 minus_product = work.tile([P, width], F32, tag="minus_product")
                 nc.vector.scalar_tensor_tensor(
                     out=minus_product[:], in0=value, scalar=-factor, in1=guess[:], op0=ALU.mult, op1=ALU.mult
                 )
+                return minus_product
+
+            def newton_result(result, minus_product, guess):
                 nc.vector.scalar_tensor_tensor(
                     out=result, in0=minus_product[:], scalar=2.0, in1=guess[:], op0=ALU.add, op1=ALU.mult
                 )
 
             def invert_norm_q(half):
                 guess = first_guess(norm_q_sb[half][:], float(D), K)
-                refine(inv_norm_q[half][:], norm_q_sb[half][:], float(D), guess, K)
+                minus_product = newton_product(norm_q_sb[half][:], float(D), guess, K)
+                newton_result(inv_norm_q[half][:], minus_product, guess)
 
             guesses = {}
-            inv_squares = {}
+            minus_products = {}
+            inv_norm_p = {}
+            inv_norm_p_sq = {}
+            grad_over_nq = {}
+            dot_over_np2 = {}
 
-            def compute_ca(n):
+            def chunk_cols(n):
+                c = n % CHUNKS
+                return slice(c * CHUNK, (c + 1) * CHUNK)
+
+            def begin_inverse(n):
+                minus_products[n] = newton_product(loaded[n][0][:], 1.0, guesses[n], CHUNK)
+
+            def finish_inverse(n):
+                inv_norm_p[n] = work.tile([P, CHUNK], F32, name="inv_norm_p", tag="inv_norm_p")
+                newton_result(inv_norm_p[n][:], minus_products[n], guesses[n])
+                inv_norm_p_sq[n] = work.tile([P, CHUNK], F32, name="inv_norm_p_sq", tag="inv_norm_p_sq")
+                nc.scalar.activation(out=inv_norm_p_sq[n][:], in_=inv_norm_p[n][:], func=ACT.Square)
+
+            def scale_gradient(n):
                 half, c = divmod(n, CHUNKS)
-                norm_p_c, grad_c, dot_c = loaded[n]
-                inv_norm_p = work.tile([P, CHUNK], F32)
-                refine(inv_norm_p[:], norm_p_c[:], 1.0, guesses[n], CHUNK)
-                inv_norm_p_sq = work.tile([P, CHUNK], F32)
-                nc.scalar.activation(out=inv_norm_p_sq[:], in_=inv_norm_p[:], func=ACT.Square)
-                inv_squares[n] = inv_norm_p_sq
-                grad_over_nq = work.tile([P, CHUNK_K, S], F32)
+                grad_over_nq[n] = work.tile([P, CHUNK_K, S], F32, name="grad_over_nq", tag="grad_over_nq")
                 nc.vector.tensor_tensor(
-                    out=grad_over_nq[:],
-                    in0=grad_c[:].rearrange("b (k s) -> b k s", s=S),
+                    out=grad_over_nq[n][:],
+                    in0=loaded[n][1][:].rearrange("b (k s) -> b k s", s=S),
                     in1=inv_norm_q[half][:, c * CHUNK_K : (c + 1) * CHUNK_K].unsqueeze(2).to_broadcast([P, CHUNK_K, S]),
                     op=ALU.mult,
                 )
+
+            def compute_ca(n):
                 nc.vector.scalar_tensor_tensor(
-                    out=ca[half][:, c * CHUNK : (c + 1) * CHUNK],
-                    in0=grad_over_nq[:].rearrange("b k s -> b (k s)"),
+                    out=ca[n // CHUNKS][:, chunk_cols(n)],
+                    in0=grad_over_nq[n][:].rearrange("b k s -> b (k s)"),
                     scalar=-1.0,
-                    in1=inv_norm_p[:],
+                    in1=inv_norm_p[n][:],
                     op0=ALU.mult,
                     op1=ALU.mult,
                 )
 
+            def divide_dot(n):
+                dot_over_np2[n] = work.tile([P, CHUNK], F32, name="dot_over_np2", tag="dot_over_np2")
+                nc.vector.tensor_tensor(
+                    out=dot_over_np2[n][:], in0=loaded[n][2][:], in1=inv_norm_p_sq[n][:], op=ALU.mult
+                )
+
             def compute_cb(n):
-                half, c = divmod(n, CHUNKS)
-                norm_p_c, grad_c, dot_c = loaded[n]
-                dot_over_np2 = work.tile([P, CHUNK], F32)
-                nc.vector.tensor_tensor(out=dot_over_np2[:], in0=dot_c[:], in1=inv_squares[n][:], op=ALU.mult)
                 nc.vector.scalar_tensor_tensor(
-                    out=cb[half][:, c * CHUNK : (c + 1) * CHUNK],
-                    in0=ca[half][:, c * CHUNK : (c + 1) * CHUNK],
+                    out=cb[n // CHUNKS][:, chunk_cols(n)],
+                    in0=ca[n // CHUNKS][:, chunk_cols(n)],
                     scalar=-1.0,
-                    in1=dot_over_np2[:],
+                    in1=dot_over_np2[n][:],
                     op0=ALU.mult,
                     op1=ALU.mult,
                 )
@@ -168,30 +189,37 @@ def tile_mpl_t_v_kernel(tc, p, q, W, dot, norm_p, norm_q, grad_out, out):
 
             invert_norm_q(0)
             guesses[0] = first_guess(loaded[0][0][:], 1.0, CHUNK)
-            for n in range(HALVES * CHUNKS):
-                half, c = divmod(n, CHUNKS)
-                if n + LOADS_AHEAD < HALVES * CHUNKS:
+            for n in range(ALL_CHUNKS + 1):
+                if n + LOADS_AHEAD < ALL_CHUNKS:
                     load_chunk(n + LOADS_AHEAD)
-                if n + 1 < HALVES * CHUNKS:
+                if n + 1 < ALL_CHUNKS:
                     guesses[n + 1] = first_guess(loaded[n + 1][0][:], 1.0, CHUNK)
-                if half == 1:
-                    turn(0, 2 * c)
-                compute_ca(n)
-                if half == 0:
-                    d_cols = slice(c * (D // CHUNKS), (c + 1) * (D // CHUNKS))
+                if n < ALL_CHUNKS:
+                    begin_inverse(n)
+                    scale_gradient(n)
+                    finish_inverse(n)
+                if n > 0:
+                    divide_dot(n - 1)
+                if n < ALL_CHUNKS:
+                    compute_ca(n)
+                if n > 0:
+                    compute_cb(n - 1)
+                if n == 0:
+                    invert_norm_q(1)
+                if n < CHUNKS:
+                    d_cols = slice(n * (D // CHUNKS), (n + 1) * (D // CHUNKS))
                     nc.scalar.activation(
                         out=w2_grouped[:, d_cols, :],
                         in_=w_rows[:, :, d_cols].rearrange("i j d -> i d j"),
                         func=ACT.Square,
                     )
-                else:
-                    turn(0, 2 * c + 1)
-                compute_cb(n)
-                if n == 0:
-                    invert_norm_q(1)
-                if half == 1:
-                    quantise(0, 2 * c)
-                    quantise(0, 2 * c + 1)
+                if n > CHUNKS:
+                    tiles_a_round = S // CHUNKS
+                    packed_now = range((n - CHUNKS - 1) * tiles_a_round, (n - CHUNKS) * tiles_a_round)
+                    for s in packed_now:
+                        turn(0, s)
+                    for s in packed_now:
+                        quantise(0, s)
             nc.vector.quantize_mx(
                 out=w2_codes[:].bitcast(E4M3_X4),
                 scales=w2_scales[:],
@@ -199,8 +227,8 @@ def tile_mpl_t_v_kernel(tc, p, q, W, dot, norm_p, norm_q, grad_out, out):
             )
 
 
-        terms = whole.enter_context(tc.tile_pool(name="terms", bufs=4))
-        order = [(half, s) for s in range(S) for half in halves]
+        terms = whole.enter_context(tc.tile_pool(name="terms", bufs=6))
+        order = [(0, 0)] + [tile for s in range(1, S) for tile in ((0, s), (1, s - 1))] + [(1, S - 1)]
         p_tiles = {}
 
         def load_p(n):
@@ -232,19 +260,17 @@ def tile_mpl_t_v_kernel(tc, p, q, W, dot, norm_p, norm_q, grad_out, out):
                     )
                 nc.vector.tensor_tensor(out=q_term[:, d_cols], in0=m1[:], in1=q_last[half][:, d_cols], op=ALU.mult)
                 nc.vector.tensor_tensor(out=p_term[:, d_cols], in0=m2[:], in1=p_tile[:, d_cols], op=ALU.mult)
-            nc.gpsimd.tensor_tensor(out=q_term[:], in0=q_term[:], in1=p_term[:], op=ALU.add)
+            adder = nc.gpsimd if n + 1 < len(order) else nc.vector
+            adder.tensor_tensor(out=q_term[:], in0=q_term[:], in1=p_term[:], op=ALU.add)
             nc.sync.dma_start(out=out[batch_rows(half), s, :], in_=q_term[:])
 
         for half in halves:
             nc.sync.dma_start(out=q_last[half][:], in_=q[batch_rows(half), S - 1, :])
         for n in range(P_AHEAD):
             load_p(n)
-        turn(1, 0)
-        quantise(1, 0)
-        for s in range(S):
-            if s + 1 < S:
-                turn(1, s + 1)
-            write_output(2 * s)
-            if s + 1 < S:
-                quantise(1, s + 1)
-            write_output(2 * s + 1)
+        for n, (half, s) in enumerate(order):
+            if half == 0:
+                turn(1, s)
+            write_output(n)
+            if half == 0:
+                quantise(1, s)

@@ -21,7 +21,10 @@ CHUNK = CHUNK_K * S
 CHUNKS = K // CHUNK_K
 N_COLS = 512
 ALL_CHUNKS = HALVES * CHUNKS
+TILES_A_ROUND = S // CHUNKS
 LOADS_AHEAD = 2
+GROUP = 4
+LAG = GROUP + 1
 P_AHEAD = 3
 
 FLOPS = 2 * 2 * B * S * K * D
@@ -62,21 +65,24 @@ def tile_mpl_t_v_kernel(tc, p, q, W, dot, norm_p, norm_q, grad_out, out):
         grouped_tiles = {}
 
         def turn(half, s):
-            grouped = grouped_pool.tile([P, 2, P, PACK], BF16, align_bytes=64)
+            if s % GROUP == 0:
+                grouped_tiles[(half, s // GROUP)] = grouped_pool.tile(
+                    [P, GROUP, 2, P, PACK], BF16, name="grouped", tag="grouped", align_bytes=64
+                )
+            grouped = grouped_tiles[(half, s // GROUP)]
             for which, coefficient in enumerate((ca[half], cb[half])):
                 by_k = coefficient[:].rearrange("b (i j s) -> b j s i", j=PACK, s=S)
                 turned = turned_pool.tile([P, PACK, P], F32)
                 for j in range(PACK):
                     nc.tensor.transpose(turned[:, j, :], by_k[:, j, s, :], identity[:])
-                nc.scalar.copy(out=grouped[:, which], in_=turned[:].rearrange("i j b -> i b j"))
-            grouped_tiles[(half, s)] = grouped
+                nc.scalar.copy(out=grouped[:, s % GROUP, which], in_=turned[:].rearrange("i j b -> i b j"))
 
-        def quantise(half, s):
-            grouped = grouped_tiles[(half, s)]
+        def quantise_group_ending_at(half, s):
+            group = slice(s + 1 - GROUP, s + 1)
             nc.vector.quantize_mx(
-                out=codes[half][:, s, :].bitcast(E5M2_X4),
-                scales=scales[half][:, s, :],
-                in_=grouped[:].rearrange("i c b j -> i (c b j)"),
+                out=codes[half][:, group, :].rearrange("i s w -> i (s w)").bitcast(E5M2_X4),
+                scales=scales[half][:, group, :].rearrange("i s w -> i (s w)"),
+                in_=grouped_tiles[(half, s // GROUP)][:].rearrange("i s c b j -> i (s c b j)"),
             )
 
 
@@ -194,6 +200,9 @@ def tile_mpl_t_v_kernel(tc, p, q, W, dot, norm_p, norm_q, grad_out, out):
                     load_chunk(n + LOADS_AHEAD)
                 if n + 1 < ALL_CHUNKS:
                     guesses[n + 1] = first_guess(loaded[n + 1][0][:], 1.0, CHUNK)
+                packed_now = range(max(n - CHUNKS - 1, 0) * TILES_A_ROUND, max(n - CHUNKS, 0) * TILES_A_ROUND)
+                for s in packed_now:
+                    turn(0, s)
                 if n < ALL_CHUNKS:
                     begin_inverse(n)
                     scale_gradient(n)
@@ -213,22 +222,20 @@ def tile_mpl_t_v_kernel(tc, p, q, W, dot, norm_p, norm_q, grad_out, out):
                         in_=w_rows[:, :, d_cols].rearrange("i j d -> i d j"),
                         func=ACT.Square,
                     )
-                if n > CHUNKS:
-                    tiles_a_round = S // CHUNKS
-                    packed_now = range((n - CHUNKS - 1) * tiles_a_round, (n - CHUNKS) * tiles_a_round)
-                    for s in packed_now:
-                        turn(0, s)
-                    for s in packed_now:
-                        quantise(0, s)
-            nc.vector.quantize_mx(
-                out=w2_codes[:].bitcast(E4M3_X4),
-                scales=w2_scales[:],
-                in_=w2_grouped[:].rearrange("i d j -> i (d j)"),
-            )
+                if n == CHUNKS:
+                    nc.vector.quantize_mx(
+                        out=w2_codes[:].bitcast(E4M3_X4),
+                        scales=w2_scales[:],
+                        in_=w2_grouped[:].rearrange("i d j -> i (d j)"),
+                    )
+                for s in packed_now:
+                    if s % GROUP == GROUP - 1:
+                        quantise_group_ending_at(0, s)
 
 
         terms = whole.enter_context(tc.tile_pool(name="terms", bufs=6))
-        order = [(0, 0)] + [tile for s in range(1, S) for tile in ((0, s), (1, s - 1))] + [(1, S - 1)]
+        steps = range(S + LAG)
+        order = [tile for s in steps for tile in ((0, s), (1, s - LAG)) if 0 <= tile[1] < S]
         p_tiles = {}
 
         def load_p(n):
@@ -238,8 +245,8 @@ def tile_mpl_t_v_kernel(tc, p, q, W, dot, norm_p, norm_q, grad_out, out):
                 nc.sync.dma_start(out=p_tile[:], in_=p[batch_rows(half), s, :])
                 p_tiles[n] = p_tile
 
-        def write_output(n):
-            half, s = order[n]
+        def write_output(half, s):
+            n = order.index((half, s))
             load_p(n + P_AHEAD)
             p_tile = p_tiles[n]
             q_term = terms.tile([P, D], F32)
@@ -268,9 +275,11 @@ def tile_mpl_t_v_kernel(tc, p, q, W, dot, norm_p, norm_q, grad_out, out):
             nc.sync.dma_start(out=q_last[half][:], in_=q[batch_rows(half), S - 1, :])
         for n in range(P_AHEAD):
             load_p(n)
-        for n, (half, s) in enumerate(order):
-            if half == 0:
+        for s in steps:
+            if s < S:
+                write_output(0, s)
                 turn(1, s)
-            write_output(n)
-            if half == 0:
-                quantise(1, s)
+            if 0 < s <= S and s % GROUP == 0:
+                quantise_group_ending_at(1, s - 1)
+            if s >= LAG:
+                write_output(1, s - LAG)

@@ -16,16 +16,12 @@ B, S, D, K = 256, 8, 1024, 512
 P = 128
 PACK = 4
 HALVES = B // P
-CHUNK_K = 128
-CHUNK = CHUNK_K * S
-CHUNKS = K // CHUNK_K
+UNITS = HALVES * S
 N_COLS = 512
-ALL_CHUNKS = HALVES * CHUNKS
-TILES_A_ROUND = S // CHUNKS
-LOADS_AHEAD = 2
-GROUP = 4
-LAG = GROUP + 1
-P_AHEAD = 3
+D_HALVES = D // N_COLS
+MX_LAG = 2
+OUT_LAG = MX_LAG + 1
+P_AHEAD = 4
 
 FLOPS = 2 * 2 * B * S * K * D
 BYTES = 2 * (B * S * D + B * D + K * D + B * S * K) + 4 * (2 * B * K * S + B * K + B * S * D)
@@ -40,246 +36,281 @@ def tile_mpl_t_v_kernel(tc, p, q, W, dot, norm_p, norm_q, grad_out, out):
     with ExitStack() as whole:
         whole.enter_context(tc.manual_schedule())
         keep = whole.enter_context(tc.tile_pool(name="keep", bufs=1))
-        grouped_pool = whole.enter_context(tc.tile_pool(name="grouped", bufs=2))
+        mid = whole.enter_context(tc.tile_pool(name="mid", bufs=3))
+        packed = whole.enter_context(tc.tile_pool(name="packed", bufs=3))
         p_pool = whole.enter_context(tc.tile_pool(name="p_rows", bufs=P_AHEAD + 1))
-        turned_pool = whole.enter_context(tc.psum_pool(name="turned", bufs=4))
+        terms = whole.enter_context(tc.tile_pool(name="terms", bufs=3))
+        turned_pool = whole.enter_context(tc.psum_pool(name="turned", bufs=1))
         product_pool = whole.enter_context(tc.psum_pool(name="product", bufs=2))
 
+        halves = range(HALVES)
         identity = keep.tile([P, P], F32)
         make_identity(nc, identity[:])
+        one = keep.tile([P, 1], F32)
+        nc.vector.memset(one[:], 1.0)
+        warm = keep.tile([P, 1], F32)
+        nc.scalar.activation(out=warm[:], in_=one[:], func=ACT.Abs_reciprocal_sqrt)
+
+        w_rows = keep.tile([P, PACK, D], BF16)
+        w2_grouped = keep.tile([P, D, PACK], BF16, align_bytes=64)
         w2_codes = keep.tile([P, D], U32, align_bytes=64)
         w2_scales = keep.tile([P, D], U8, align_bytes=64)
-        halves = range(HALVES)
         norm_q_sb = [keep.tile([P, K], F32, name="norm_q_sb%d" % h) for h in halves]
-        inv_norm_q = [keep.tile([P, K], F32, name="inv_norm_q%d" % h) for h in halves]
+        minus_inv_norm_q = [keep.tile([P, K], F32, name="minus_inv_norm_q%d" % h) for h in halves]
         q_last = [keep.tile([P, D], BF16, name="q_last%d" % h) for h in halves]
-        ca = [keep.tile([P, K * S], F32, name="ca%d" % h) for h in halves]
-        cb = [keep.tile([P, K * S], F32, name="cb%d" % h) for h in halves]
-        codes = [keep.tile([P, S, 2 * P], U32, name="codes%d" % h, align_bytes=64) for h in halves]
-        scales = [keep.tile([P, S, 2 * P], U8, name="scales%d" % h, align_bytes=64) for h in halves]
+        norm_p_sb = [keep.tile([P, K * S], F32, name="norm_p_sb%d" % h) for h in halves]
+        dot_sb = [keep.tile([P, K * S], F32, name="dot_sb%d" % h) for h in halves]
+        grad_sb = [keep.tile([P, K * S], BF16, name="grad_sb%d" % h) for h in halves]
 
         def batch_rows(half):
             return slice(half * P, (half + 1) * P)
 
-
-        grouped_tiles = {}
-
-        def turn(half, s):
-            if s % GROUP == 0:
-                grouped_tiles[(half, s // GROUP)] = grouped_pool.tile(
-                    [P, GROUP, 2, P, PACK], BF16, name="grouped", tag="grouped", align_bytes=64
-                )
-            grouped = grouped_tiles[(half, s // GROUP)]
-            for which, coefficient in enumerate((ca[half], cb[half])):
-                by_k = coefficient[:].rearrange("b (i j s) -> b j s i", j=PACK, s=S)
-                turned = turned_pool.tile([P, PACK, P], F32)
-                for j in range(PACK):
-                    nc.tensor.transpose(turned[:, j, :], by_k[:, j, s, :], identity[:])
-                nc.scalar.copy(out=grouped[:, s % GROUP, which], in_=turned[:].rearrange("i j b -> i b j"))
-
-        def quantise_group_ending_at(half, s):
-            group = slice(s + 1 - GROUP, s + 1)
-            nc.vector.quantize_mx(
-                out=codes[half][:, group, :].rearrange("i s w -> i (s w)").bitcast(E5M2_X4),
-                scales=scales[half][:, group, :].rearrange("i s w -> i (s w)"),
-                in_=grouped_tiles[(half, s // GROUP)][:].rearrange("i s c b j -> i (s c b j)"),
-            )
+        def in_range(u):
+            return 0 <= u < UNITS
 
 
-        with ExitStack() as coefficient_phase:
-            inputs = coefficient_phase.enter_context(tc.tile_pool(name="inputs", bufs=LOADS_AHEAD + 1))
-            work = coefficient_phase.enter_context(tc.tile_pool(name="work", bufs=2))
-            w_pool = coefficient_phase.enter_context(tc.tile_pool(name="w", bufs=1))
+        def load_half(half):
+            nc.sync.dma_start(out=norm_p_sb[half][:], in_=norm_p_rows[batch_rows(half), :])
+            nc.sync.dma_start(out=grad_sb[half][:], in_=grad_rows[batch_rows(half), :])
+            nc.sync.dma_start(out=dot_sb[half][:], in_=dot_rows[batch_rows(half), :])
+            nc.sync.dma_start(out=q_last[half][:], in_=q[batch_rows(half), S - 1, :])
 
-            loaded = {}
-
-            def load_chunk(n):
-                half, c = divmod(n, CHUNKS)
-                cols = slice(c * CHUNK, (c + 1) * CHUNK)
-                norm_p_c = inputs.tile([P, CHUNK], F32)
-                nc.sync.dma_start(out=norm_p_c[:], in_=norm_p_rows[batch_rows(half), cols])
-                grad_c = inputs.tile([P, CHUNK], BF16)
-                nc.sync.dma_start(out=grad_c[:], in_=grad_rows[batch_rows(half), cols])
-                dot_c = inputs.tile([P, CHUNK], F32)
-                nc.sync.dma_start(out=dot_c[:], in_=dot_rows[batch_rows(half), cols])
-                loaded[n] = (norm_p_c, grad_c, dot_c)
-
-            def first_guess(value, factor, width):
-                squared = work.tile([P, width], F32, tag="squared")
-                nc.scalar.activation(out=squared[:], in_=value, func=ACT.Square, scale=factor)
-                guess = work.tile([P, width], F32, tag="guess", bufs=3)
-                nc.scalar.activation(out=guess[:], in_=squared[:], func=ACT.Abs_reciprocal_sqrt)
-                return guess
-
-
-            def newton_product(value, factor, guess, width):
-                minus_product = work.tile([P, width], F32, tag="minus_product")
-                nc.vector.scalar_tensor_tensor(
-                    out=minus_product[:], in0=value, scalar=-factor, in1=guess[:], op0=ALU.mult, op1=ALU.mult
-                )
-                return minus_product
-
-            def newton_result(result, minus_product, guess):
-                nc.vector.scalar_tensor_tensor(
-                    out=result, in0=minus_product[:], scalar=2.0, in1=guess[:], op0=ALU.add, op1=ALU.mult
-                )
-
-            def invert_norm_q(half):
-                guess = first_guess(norm_q_sb[half][:], float(D), K)
-                minus_product = newton_product(norm_q_sb[half][:], float(D), guess, K)
-                newton_result(inv_norm_q[half][:], minus_product, guess)
-
-            guesses = {}
-            minus_products = {}
-            inv_norm_p = {}
-            inv_norm_p_sq = {}
-            grad_over_nq = {}
-            dot_over_np2 = {}
-
-            def chunk_cols(n):
-                c = n % CHUNKS
-                return slice(c * CHUNK, (c + 1) * CHUNK)
-
-            def begin_inverse(n):
-                minus_products[n] = newton_product(loaded[n][0][:], 1.0, guesses[n], CHUNK)
-
-            def finish_inverse(n):
-                inv_norm_p[n] = work.tile([P, CHUNK], F32, name="inv_norm_p", tag="inv_norm_p")
-                newton_result(inv_norm_p[n][:], minus_products[n], guesses[n])
-                inv_norm_p_sq[n] = work.tile([P, CHUNK], F32, name="inv_norm_p_sq", tag="inv_norm_p_sq")
-                nc.scalar.activation(out=inv_norm_p_sq[n][:], in_=inv_norm_p[n][:], func=ACT.Square)
-
-            def scale_gradient(n):
-                half, c = divmod(n, CHUNKS)
-                grad_over_nq[n] = work.tile([P, CHUNK_K, S], F32, name="grad_over_nq", tag="grad_over_nq")
-                nc.vector.tensor_tensor(
-                    out=grad_over_nq[n][:],
-                    in0=loaded[n][1][:].rearrange("b (k s) -> b k s", s=S),
-                    in1=inv_norm_q[half][:, c * CHUNK_K : (c + 1) * CHUNK_K].unsqueeze(2).to_broadcast([P, CHUNK_K, S]),
-                    op=ALU.mult,
-                )
-
-            def compute_ca(n):
-                nc.vector.scalar_tensor_tensor(
-                    out=ca[n // CHUNKS][:, chunk_cols(n)],
-                    in0=grad_over_nq[n][:].rearrange("b k s -> b (k s)"),
-                    scalar=-1.0,
-                    in1=inv_norm_p[n][:],
-                    op0=ALU.mult,
-                    op1=ALU.mult,
-                )
-
-            def divide_dot(n):
-                dot_over_np2[n] = work.tile([P, CHUNK], F32, name="dot_over_np2", tag="dot_over_np2")
-                nc.vector.tensor_tensor(
-                    out=dot_over_np2[n][:], in0=loaded[n][2][:], in1=inv_norm_p_sq[n][:], op=ALU.mult
-                )
-
-            def compute_cb(n):
-                nc.vector.scalar_tensor_tensor(
-                    out=cb[n // CHUNKS][:, chunk_cols(n)],
-                    in0=ca[n // CHUNKS][:, chunk_cols(n)],
-                    scalar=-1.0,
-                    in1=dot_over_np2[n][:],
-                    op0=ALU.mult,
-                    op1=ALU.mult,
-                )
-
-            nc.sync.dma_start(out=norm_q_sb[0][:], in_=norm_q[batch_rows(0), :])
-            for n in range(LOADS_AHEAD):
-                load_chunk(n)
-            nc.sync.dma_start(out=norm_q_sb[1][:], in_=norm_q[batch_rows(1), :])
-            w_rows = w_pool.tile([P, PACK, D], BF16)
-            nc.sync.dma_start(out=w_rows[:], in_=W.rearrange("(i j) d -> i j d", j=PACK))
-            w2_grouped = w_pool.tile([P, D, PACK], BF16, align_bytes=64)
-
-            invert_norm_q(0)
-            guesses[0] = first_guess(loaded[0][0][:], 1.0, CHUNK)
-            for n in range(ALL_CHUNKS + 1):
-                if n + LOADS_AHEAD < ALL_CHUNKS:
-                    load_chunk(n + LOADS_AHEAD)
-                if n + 1 < ALL_CHUNKS:
-                    guesses[n + 1] = first_guess(loaded[n + 1][0][:], 1.0, CHUNK)
-                packed_now = range(max(n - CHUNKS - 1, 0) * TILES_A_ROUND, max(n - CHUNKS, 0) * TILES_A_ROUND)
-                for s in packed_now:
-                    turn(0, s)
-                if n < ALL_CHUNKS:
-                    begin_inverse(n)
-                    scale_gradient(n)
-                    finish_inverse(n)
-                if n > 0:
-                    divide_dot(n - 1)
-                if n < ALL_CHUNKS:
-                    compute_ca(n)
-                if n > 0:
-                    compute_cb(n - 1)
-                if n == 0:
-                    invert_norm_q(1)
-                if n < CHUNKS:
-                    d_cols = slice(n * (D // CHUNKS), (n + 1) * (D // CHUNKS))
-                    nc.scalar.activation(
-                        out=w2_grouped[:, d_cols, :],
-                        in_=w_rows[:, :, d_cols].rearrange("i j d -> i d j"),
-                        func=ACT.Square,
-                    )
-                if n == CHUNKS:
-                    nc.vector.quantize_mx(
-                        out=w2_codes[:].bitcast(E4M3_X4),
-                        scales=w2_scales[:],
-                        in_=w2_grouped[:].rearrange("i d j -> i (d j)"),
-                    )
-                for s in packed_now:
-                    if s % GROUP == GROUP - 1:
-                        quantise_group_ending_at(0, s)
-
-
-        terms = whole.enter_context(tc.tile_pool(name="terms", bufs=6))
-        steps = range(S + LAG)
-        order = [tile for s in steps for tile in ((0, s), (1, s - LAG)) if 0 <= tile[1] < S]
         p_tiles = {}
 
-        def load_p(n):
-            if n < len(order):
-                half, s = order[n]
-                p_tile = p_pool.tile([P, D], BF16)
-                nc.sync.dma_start(out=p_tile[:], in_=p[batch_rows(half), s, :])
-                p_tiles[n] = p_tile
+        def load_p(u):
+            if in_range(u):
+                half, s = divmod(u, S)
+                p_tiles[u] = p_pool.tile([P, D], BF16, name="p_tile", tag="p_tile")
+                nc.sync.dma_start(out=p_tiles[u][:], in_=p[batch_rows(half), s, :])
 
-        def write_output(half, s):
-            n = order.index((half, s))
-            load_p(n + P_AHEAD)
-            p_tile = p_tiles[n]
-            q_term = terms.tile([P, D], F32)
-            p_term = terms.tile([P, D], F32)
-            for d_cols in (slice(0, N_COLS), slice(N_COLS, D)):
-                m1 = product_pool.tile([P, N_COLS], F32)
-                m2 = product_pool.tile([P, N_COLS], F32)
+        nc.sync.dma_start(out=w_rows[:], in_=W.rearrange("(i j) d -> i j d", j=PACK))
+        for half in halves:
+            nc.sync.dma_start(out=norm_q_sb[half][:], in_=norm_q[batch_rows(half), :])
+        load_half(0)
+        for u in range(P_AHEAD):
+            load_p(u)
+        load_half(1)
+
+
+        for piece in range(4):
+            d_cols = slice(piece * (D // 4), (piece + 1) * (D // 4))
+            nc.scalar.activation(
+                out=w2_grouped[:, d_cols, :],
+                in_=w_rows[:, :, d_cols].rearrange("i j d -> i d j"),
+                func=ACT.Square,
+            )
+            if piece % 2 == 1:
+                d_half = slice((piece // 2) * N_COLS, (piece // 2 + 1) * N_COLS)
+                nc.vector.quantize_mx(
+                    out=w2_codes[:, d_half].bitcast(E4M3_X4),
+                    scales=w2_scales[:, d_half],
+                    in_=w2_grouped[:, d_half, :].rearrange("i d j -> i (d j)"),
+                )
+
+
+        def by_token(turned):
+            return turned[:].rearrange("i j b -> i b j")
+
+        def turn(name, columns):
+            turned = turned_pool.tile([P, PACK, P], F32, name=name, tag=name)
+            for j in range(PACK):
+                nc.tensor.transpose(turned[:, j, :], columns(j), identity[:])
+            return turned
+
+        inv_norm_q_turned = {}
+
+        def invert_norm_q(half):
+            root = mid.tile([P, K], F32, name="root_q", tag="root")
+            nc.scalar.activation(out=root[:], in_=norm_q_sb[half][:], func=ACT.Abs_reciprocal_sqrt, scale=float(D))
+            guess_q = mid.tile([P, K], F32, name="guess_q", tag="guess")
+            nc.scalar.activation(out=guess_q[:], in_=root[:], func=ACT.Square)
+            product = mid.tile([P, K], F32, name="product_q", tag="residual")
+            nc.vector.scalar_tensor_tensor(
+                out=product[:], in0=norm_q_sb[half][:], scalar=float(D), in1=guess_q[:], op0=ALU.mult, op1=ALU.mult
+            )
+            nc.vector.scalar_tensor_tensor(
+                out=minus_inv_norm_q[half][:], in0=product[:], scalar=-2.0, in1=guess_q[:], op0=ALU.add, op1=ALU.mult
+            )
+
+        def turn_inv_norm_q(half):
+            view = minus_inv_norm_q[half][:].rearrange("b (i j) -> b j i", j=PACK)
+            inv_norm_q_turned[half] = turn("inv_norm_q_turned", lambda j: view[:, j, :])
+
+        norm_p_turned = {}
+        dot_turned = {}
+        grad_turned = {}
+        guesses = {}
+        residuals = {}
+        corrections = {}
+        inverses = {}
+        inverse_squares = {}
+        ratios = {}
+        ca_f32 = {}
+        grouped = {}
+        codes = {}
+        scales = {}
+        products = {}
+        q_terms = {}
+        p_terms = {}
+
+        def mid_tile(name):
+            return mid.tile([P, P, PACK], F32, name=name, tag=name)
+
+        def turn_norm_p(u):
+            if in_range(u):
+                half, s = divmod(u, S)
+                view = norm_p_sb[half][:].rearrange("b (i j s) -> b j s i", j=PACK, s=S)
+                norm_p_turned[u] = turn("norm_p_turned", lambda j: view[:, j, s, :])
+
+        def turn_dot(u):
+            if in_range(u):
+                half, s = divmod(u, S)
+                view = dot_sb[half][:].rearrange("b (i j s) -> b j s i", j=PACK, s=S)
+                dot_turned[u] = turn("dot_turned", lambda j: view[:, j, s, :])
+
+        def turn_grad(u):
+            if in_range(u) and u % 2 == 0:
+                half, s = divmod(u, S)
+                view = grad_sb[half][:].bitcast(F32).rearrange("b (i j v) -> b j v i", j=PACK, v=S // 2)
+                grad_turned[u // 2] = turn("grad_turned", lambda j: view[:, j, s // 2, :])
+
+        def guess(u):
+            if in_range(u):
+                root = mid_tile("root")
+                nc.scalar.activation(out=root[:], in_=by_token(norm_p_turned[u]), func=ACT.Abs_reciprocal_sqrt)
+                guesses[u] = mid_tile("guess")
+                nc.scalar.activation(out=guesses[u][:], in_=root[:], func=ACT.Square)
+
+        def residual(u):
+            if in_range(u):
+                residuals[u] = mid_tile("residual")
+                nc.vector.tensor_tensor(
+                    out=residuals[u][:], in0=by_token(norm_p_turned[u]), in1=guesses[u][:], op=ALU.mult
+                )
+
+        def correction(u):
+            if in_range(u):
+                corrections[u] = mid_tile("correction")
+                nc.scalar.activation(out=corrections[u][:], in_=residuals[u][:], func=ACT.Copy, scale=-1.0, bias=2.0)
+
+        def inverse(u):
+            if in_range(u):
+                inverses[u] = mid_tile("inverse")
+                nc.gpsimd.tensor_tensor(out=inverses[u][:], in0=corrections[u][:], in1=guesses[u][:], op=ALU.mult)
+
+        def square_inverse(u):
+            if in_range(u):
+                inverse_squares[u] = mid_tile("inverse_square")
+                nc.scalar.activation(out=inverse_squares[u][:], in_=inverses[u][:], func=ACT.Square)
+
+        def coefficients(u):
+            if in_range(u):
+                half, s = divmod(u, S)
+                grad_view = (
+                    grad_turned[u // 2][:]
+                    .rearrange("i j b -> i (j b)")
+                    .bitcast(BF16)
+                    .rearrange("i (j b e) -> i e b j", j=PACK, e=2)
+                )
+                grad_over_np = mid_tile("grad_over_np")
+                nc.vector.tensor_tensor(out=grad_over_np[:], in0=grad_view[:, s % 2], in1=inverses[u][:], op=ALU.mult)
+                ratios[u] = mid_tile("ratio")
+                nc.vector.scalar_tensor_tensor(
+                    out=ratios[u][:],
+                    in0=by_token(dot_turned[u]),
+                    scalar=-1.0,
+                    in1=inverse_squares[u][:],
+                    op0=ALU.mult,
+                    op1=ALU.mult,
+                )
+                ca_f32[u] = mid_tile("ca_f32")
+                nc.vector.tensor_tensor(
+                    out=ca_f32[u][:], in0=grad_over_np[:], in1=by_token(inv_norm_q_turned[half]), op=ALU.mult
+                )
+
+        def round_ca(u):
+            if in_range(u):
+                grouped[u] = packed.tile([P, 2, P, PACK], BF16, name="grouped", tag="grouped", align_bytes=64)
+                nc.scalar.copy(out=grouped[u][:, 0], in_=ca_f32[u][:])
+
+        def compute_cb(u):
+            if in_range(u):
+                nc.gpsimd.tensor_tensor(out=grouped[u][:, 1], in0=ca_f32[u][:], in1=ratios[u][:], op=ALU.mult)
+
+        def quantise(u):
+            if in_range(u):
+                codes[u] = packed.tile([P, 2 * P], U32, name="codes", tag="codes", align_bytes=64)
+                scales[u] = packed.tile([P, 2 * P], U8, name="scales", tag="scales", align_bytes=64)
+                nc.vector.quantize_mx(
+                    out=codes[u][:].bitcast(E5M2_X4),
+                    scales=scales[u][:],
+                    in_=grouped[u][:].rearrange("i c b j -> i (c b j)"),
+                )
+
+        def d_columns(d_half):
+            return slice(d_half * N_COLS, (d_half + 1) * N_COLS)
+
+        def multiply_mx(u, d_half):
+            if in_range(u):
+                m1 = product_pool.tile([P, N_COLS], F32, name="m1", tag="m1")
+                m2 = product_pool.tile([P, N_COLS], F32, name="m2", tag="m2")
                 for which, product in enumerate((m1, m2)):
                     tokens = slice(which * P, (which + 1) * P)
                     nc.tensor.matmul_mx(
                         out=product[:],
-                        lhsT=codes[half][:, s, tokens].bitcast(E5M2_X4),
-                        lhsT_scale=scales[half][:, s, tokens],
-                        rhs=w2_codes[:, d_cols].bitcast(E4M3_X4),
-                        rhs_scale=w2_scales[:, d_cols],
+                        lhsT=codes[u][:, tokens].bitcast(E5M2_X4),
+                        lhsT_scale=scales[u][:, tokens],
+                        rhs=w2_codes[:, d_columns(d_half)].bitcast(E4M3_X4),
+                        rhs_scale=w2_scales[:, d_columns(d_half)],
                         start=True,
                         stop=True,
                     )
-                nc.vector.tensor_tensor(out=q_term[:, d_cols], in0=m1[:], in1=q_last[half][:, d_cols], op=ALU.mult)
-                nc.vector.tensor_tensor(out=p_term[:, d_cols], in0=m2[:], in1=p_tile[:, d_cols], op=ALU.mult)
-            adder = nc.gpsimd if n + 1 < len(order) else nc.vector
-            adder.tensor_tensor(out=q_term[:], in0=q_term[:], in1=p_term[:], op=ALU.add)
-            nc.sync.dma_start(out=out[batch_rows(half), s, :], in_=q_term[:])
+                products[(u, d_half)] = (m1, m2)
 
-        for half in halves:
-            nc.sync.dma_start(out=q_last[half][:], in_=q[batch_rows(half), S - 1, :])
-        for n in range(P_AHEAD):
-            load_p(n)
-        for s in steps:
-            if s < S:
-                write_output(0, s)
-                turn(1, s)
-            if 0 < s <= S and s % GROUP == 0:
-                quantise_group_ending_at(1, s - 1)
-            if s >= LAG:
-                write_output(1, s - LAG)
+        def weigh(u, d_half):
+            if in_range(u):
+                if d_half == 0:
+                    q_terms[u] = terms.tile([P, D], F32, name="q_term", tag="q_term")
+                    p_terms[u] = terms.tile([P, D], F32, name="p_term", tag="p_term")
+                cols = d_columns(d_half)
+                m1, m2 = products[(u, d_half)]
+                nc.vector.tensor_tensor(out=q_terms[u][:, cols], in0=m1[:], in1=q_last[u // S][:, cols], op=ALU.mult)
+                nc.vector.tensor_tensor(out=p_terms[u][:, cols], in0=m2[:], in1=p_tiles[u][:, cols], op=ALU.mult)
+                if d_half == D_HALVES - 1:
+                    load_p(u + P_AHEAD)
+
+        def add_terms(u, d_half):
+            if in_range(u):
+                cols = d_columns(d_half)
+                adder = nc.vector if (u == UNITS - 1 and d_half == D_HALVES - 1) else nc.gpsimd
+                adder.tensor_tensor(out=q_terms[u][:, cols], in0=q_terms[u][:, cols], in1=p_terms[u][:, cols], op=ALU.add)
+                if d_half == D_HALVES - 1:
+                    half, s = divmod(u, S)
+                    nc.sync.dma_start(out=out[batch_rows(half), s, :], in_=q_terms[u][:])
+
+        invert_norm_q(0)
+        turn_inv_norm_q(0)
+
+        for t in range(-1, UNITS + OUT_LAG + 1):
+            residual(t)
+            turn_norm_p(t + 1)
+            correction(t)
+            add_terms(t - OUT_LAG - 1, 1)
+            weigh(t - OUT_LAG, 0)
+            inverse(t)
+            guess(t + 1)
+            coefficients(t - 1)
+            if t - 1 == S - 1:
+                turn_inv_norm_q(1)
+            if t == 1:
+                invert_norm_q(1)
+            square_inverse(t)
+            add_terms(t - OUT_LAG, 0)
+            turn_grad(t)
+            turn_dot(t)
+            quantise(t - MX_LAG)
+            multiply_mx(t - MX_LAG, 0)
+            round_ca(t - 1)
+            compute_cb(t - 1)
+            weigh(t - OUT_LAG, 1)
+            multiply_mx(t - MX_LAG, 1)

@@ -83,29 +83,13 @@ def tile_mpl_t_v_kernel(tc, p, q, W, dot, norm_p, norm_q, grad_out, out):
                 p_tiles[u] = p_pool.tile([P, D], BF16, name="p_tile", tag="p_tile")
                 nc.sync.dma_start(out=p_tiles[u][:], in_=p[batch_rows(half), s, :])
 
+        nc.sync.dma_start(out=norm_q_sb[0][:], in_=norm_q[batch_rows(0), :])
         nc.sync.dma_start(out=w_rows[:], in_=W.rearrange("(i j) d -> i j d", j=PACK))
-        for half in halves:
-            nc.sync.dma_start(out=norm_q_sb[half][:], in_=norm_q[batch_rows(half), :])
         load_half(0)
         for u in range(P_AHEAD):
             load_p(u)
+        nc.sync.dma_start(out=norm_q_sb[1][:], in_=norm_q[batch_rows(1), :])
         load_half(1)
-
-
-        for piece in range(4):
-            d_cols = slice(piece * (D // 4), (piece + 1) * (D // 4))
-            nc.scalar.activation(
-                out=w2_grouped[:, d_cols, :],
-                in_=w_rows[:, :, d_cols].rearrange("i j d -> i d j"),
-                func=ACT.Square,
-            )
-            if piece % 2 == 1:
-                d_half = slice((piece // 2) * N_COLS, (piece // 2 + 1) * N_COLS)
-                nc.vector.quantize_mx(
-                    out=w2_codes[:, d_half].bitcast(E4M3_X4),
-                    scales=w2_scales[:, d_half],
-                    in_=w2_grouped[:, d_half, :].rearrange("i d j -> i (d j)"),
-                )
 
 
         def by_token(turned):
@@ -279,23 +263,40 @@ def tile_mpl_t_v_kernel(tc, p, q, W, dot, norm_p, norm_q, grad_out, out):
                 if d_half == D_HALVES - 1:
                     load_p(u + P_AHEAD)
 
-        def add_terms(u, d_half):
+        def add_terms(u, first_d_half, d_halves, adder):
             if in_range(u):
-                cols = d_columns(d_half)
-                adder = nc.vector if (u == UNITS - 1 and d_half == D_HALVES - 1) else nc.gpsimd
+                half, s = divmod(u, S)
+                cols = slice(first_d_half * N_COLS, (first_d_half + d_halves) * N_COLS)
                 adder.tensor_tensor(out=q_terms[u][:, cols], in0=q_terms[u][:, cols], in1=p_terms[u][:, cols], op=ALU.add)
-                if d_half == D_HALVES - 1:
-                    half, s = divmod(u, S)
-                    nc.sync.dma_start(out=out[batch_rows(half), s, :], in_=q_terms[u][:])
+                nc.sync.dma_start(out=out[batch_rows(half), s, cols], in_=q_terms[u][:, cols])
 
         invert_norm_q(0)
         turn_inv_norm_q(0)
 
-        for t in range(-1, UNITS + OUT_LAG + 1):
+
+        for piece in range(4):
+            d_cols = slice(piece * (D // 4), (piece + 1) * (D // 4))
+            nc.scalar.activation(
+                out=w2_grouped[:, d_cols, :],
+                in_=w_rows[:, :, d_cols].rearrange("i j d -> i d j"),
+                func=ACT.Square,
+            )
+            if piece % 2 == 1:
+                d_half = slice((piece // 2) * N_COLS, (piece // 2 + 1) * N_COLS)
+                nc.vector.quantize_mx(
+                    out=w2_codes[:, d_half].bitcast(E4M3_X4),
+                    scales=w2_scales[:, d_half],
+                    in_=w2_grouped[:, d_half, :].rearrange("i d j -> i (d j)"),
+                )
+
+
+        last = UNITS - 1
+        for t in range(-1, UNITS + OUT_LAG):
             residual(t)
             turn_norm_p(t + 1)
             correction(t)
-            add_terms(t - OUT_LAG - 1, 1)
+            if t - OUT_LAG - 1 != last:
+                add_terms(t - OUT_LAG - 1, 0, D_HALVES, nc.gpsimd)
             weigh(t - OUT_LAG, 0)
             inverse(t)
             guess(t + 1)
@@ -305,7 +306,8 @@ def tile_mpl_t_v_kernel(tc, p, q, W, dot, norm_p, norm_q, grad_out, out):
             if t == 1:
                 invert_norm_q(1)
             square_inverse(t)
-            add_terms(t - OUT_LAG, 0)
+            if t - OUT_LAG == last:
+                add_terms(last, 0, 1, nc.gpsimd)
             turn_grad(t)
             turn_dot(t)
             quantise(t - MX_LAG)
@@ -314,3 +316,5 @@ def tile_mpl_t_v_kernel(tc, p, q, W, dot, norm_p, norm_q, grad_out, out):
             compute_cb(t - 1)
             weigh(t - OUT_LAG, 1)
             multiply_mx(t - MX_LAG, 1)
+            if t - OUT_LAG == last:
+                add_terms(last, 1, 1, nc.vector)

from contextlib import ExitStack

import concourse.mybir as mybir
from concourse.masks import make_identity

F32 = mybir.dt.float32
BF16 = mybir.dt.bfloat16
U32 = mybir.dt.uint32
U8 = mybir.dt.uint8
E4M3_X4 = mybir.dt.float8_e4m3fn_x4
E5M2_X4 = mybir.dt.float8_e5m2_x4
ACT = mybir.ActivationFunctionType
ALU = mybir.AluOpType

B, S, D, K = 256, 8, 1024, 512
P = 128
PACK = 4
HALVES = B // P
UNITS = HALVES * S
N_COLS = 512
D_HALVES = D // N_COLS
MX_LAG = 2
OUT_LAG = MX_LAG + 1
P_AHEAD = 4

FLOPS = 2 * 2 * B * S * K * D
BYTES = 2 * (B * S * D + B * D + K * D + B * S * K) + 4 * (2 * B * K * S + B * K + B * S * D)


def tile_mpl_t_v_kernel(tc, p, q, W, dot, norm_p, norm_q, grad_out, out):
    nc = tc.nc
    dot_rows = dot.rearrange("b k s -> b (k s)")
    norm_p_rows = norm_p.rearrange("b k s -> b (k s)")
    grad_rows = grad_out.rearrange("b s k -> b (s k)")

    with ExitStack() as whole:
        whole.enter_context(tc.manual_schedule())
        keep = whole.enter_context(tc.tile_pool(name="keep", bufs=1))
        mid = whole.enter_context(tc.tile_pool(name="mid", bufs=3))
        packed = whole.enter_context(tc.tile_pool(name="packed", bufs=3))
        p_pool = whole.enter_context(tc.tile_pool(name="p_rows", bufs=P_AHEAD + 1))
        terms = whole.enter_context(tc.tile_pool(name="terms", bufs=3))
        turned_pool = whole.enter_context(tc.psum_pool(name="turned", bufs=1))
        product_pool = whole.enter_context(tc.psum_pool(name="product", bufs=2))

        halves = range(HALVES)
        identity = keep.tile([P, P], F32)
        make_identity(nc, identity[:])
        one = keep.tile([P, 1], F32)
        nc.vector.memset(one[:], 1.0)
        warm = keep.tile([P, 1], F32)
        nc.scalar.activation(out=warm[:], in_=one[:], func=ACT.Abs_reciprocal_sqrt)

        w_rows = keep.tile([P, PACK, D], BF16)
        w2_grouped = keep.tile([P, D, PACK], BF16, align_bytes=64)
        w2_codes = keep.tile([P, D], U32, align_bytes=64)
        w2_scales = keep.tile([P, D], U8, align_bytes=64)
        norm_q_sb = [keep.tile([P, K], F32, name="norm_q_sb%d" % h) for h in halves]
        minus_inv_norm_q = [keep.tile([P, K], F32, name="minus_inv_norm_q%d" % h) for h in halves]
        q_last = [keep.tile([P, D], BF16, name="q_last%d" % h) for h in halves]
        norm_p_sb = [keep.tile([P, K * S], F32, name="norm_p_sb%d" % h) for h in halves]
        dot_sb = [keep.tile([P, K * S], F32, name="dot_sb%d" % h) for h in halves]
        grad_sb = [keep.tile([P, K * S], BF16, name="grad_sb%d" % h) for h in halves]

        def batch_rows(half):
            return slice(half * P, (half + 1) * P)

        def in_range(u):
            return 0 <= u < UNITS


        def load_half(half):
            nc.sync.dma_start(out=norm_p_sb[half][:], in_=norm_p_rows[batch_rows(half), :])
            nc.sync.dma_start(out=grad_sb[half][:], in_=grad_rows[batch_rows(half), :])
            nc.sync.dma_start(out=dot_sb[half][:], in_=dot_rows[batch_rows(half), :])
            nc.sync.dma_start(out=q_last[half][:], in_=q[batch_rows(half), S - 1, :])

        p_tiles = {}

        def load_p(u):
            if in_range(u):
                half, s = divmod(u, S)
                p_tiles[u] = p_pool.tile([P, D], BF16, name="p_tile", tag="p_tile")
                nc.sync.dma_start(out=p_tiles[u][:], in_=p[batch_rows(half), s, :])

        nc.sync.dma_start(out=norm_q_sb[0][:], in_=norm_q[batch_rows(0), :])
        nc.sync.dma_start(out=w_rows[:], in_=W.rearrange("(i j) d -> i j d", j=PACK))
        load_half(0)
        for u in range(P_AHEAD):
            load_p(u)
        nc.sync.dma_start(out=norm_q_sb[1][:], in_=norm_q[batch_rows(1), :])
        load_half(1)


        def by_token(turned):
            return turned[:].rearrange("i j b -> i b j")

        def turn(name, columns):
            turned = turned_pool.tile([P, PACK, P], F32, name=name, tag=name)
            for j in range(PACK):
                nc.tensor.transpose(turned[:, j, :], columns(j), identity[:])
            return turned

        inv_norm_q_turned = {}

        def invert_norm_q(half):
            root = mid.tile([P, K], F32, name="root_q", tag="root")
            nc.scalar.activation(out=root[:], in_=norm_q_sb[half][:], func=ACT.Abs_reciprocal_sqrt, scale=float(D))
            guess_q = mid.tile([P, K], F32, name="guess_q", tag="guess")
            nc.scalar.activation(out=guess_q[:], in_=root[:], func=ACT.Square)
            product = mid.tile([P, K], F32, name="product_q", tag="residual")
            nc.vector.scalar_tensor_tensor(
                out=product[:], in0=norm_q_sb[half][:], scalar=float(D), in1=guess_q[:], op0=ALU.mult, op1=ALU.mult
            )
            nc.vector.scalar_tensor_tensor(
                out=minus_inv_norm_q[half][:], in0=product[:], scalar=-2.0, in1=guess_q[:], op0=ALU.add, op1=ALU.mult
            )

        def turn_inv_norm_q(half):
            view = minus_inv_norm_q[half][:].rearrange("b (i j) -> b j i", j=PACK)
            inv_norm_q_turned[half] = turn("inv_norm_q_turned", lambda j: view[:, j, :])

        norm_p_turned = {}
        dot_turned = {}
        grad_turned = {}
        guesses = {}
        residuals = {}
        corrections = {}
        inverses = {}
        inverse_squares = {}
        ratios = {}
        ca_f32 = {}
        grouped = {}
        codes = {}
        scales = {}
        products = {}
        q_terms = {}
        p_terms = {}

        def mid_tile(name):
            return mid.tile([P, P, PACK], F32, name=name, tag=name)

        def turn_norm_p(u):
            if in_range(u):
                half, s = divmod(u, S)
                view = norm_p_sb[half][:].rearrange("b (i j s) -> b j s i", j=PACK, s=S)
                norm_p_turned[u] = turn("norm_p_turned", lambda j: view[:, j, s, :])

        def turn_dot(u):
            if in_range(u):
                half, s = divmod(u, S)
                view = dot_sb[half][:].rearrange("b (i j s) -> b j s i", j=PACK, s=S)
                dot_turned[u] = turn("dot_turned", lambda j: view[:, j, s, :])

        def turn_grad(u):
            if in_range(u) and u % 2 == 0:
                half, s = divmod(u, S)
                view = grad_sb[half][:].bitcast(F32).rearrange("b (i j v) -> b j v i", j=PACK, v=S // 2)
                grad_turned[u // 2] = turn("grad_turned", lambda j: view[:, j, s // 2, :])

        def guess(u):
            if in_range(u):
                root = mid_tile("root")
                nc.scalar.activation(out=root[:], in_=by_token(norm_p_turned[u]), func=ACT.Abs_reciprocal_sqrt)
                guesses[u] = mid_tile("guess")
                nc.scalar.activation(out=guesses[u][:], in_=root[:], func=ACT.Square)

        def residual(u):
            if in_range(u):
                residuals[u] = mid_tile("residual")
                nc.vector.tensor_tensor(
                    out=residuals[u][:], in0=by_token(norm_p_turned[u]), in1=guesses[u][:], op=ALU.mult
                )

        def correction(u):
            if in_range(u):
                corrections[u] = mid_tile("correction")
                nc.scalar.activation(out=corrections[u][:], in_=residuals[u][:], func=ACT.Copy, scale=-1.0, bias=2.0)

        def inverse(u):
            if in_range(u):
                inverses[u] = mid_tile("inverse")
                nc.gpsimd.tensor_tensor(out=inverses[u][:], in0=corrections[u][:], in1=guesses[u][:], op=ALU.mult)

        def square_inverse(u):
            if in_range(u):
                inverse_squares[u] = mid_tile("inverse_square")
                nc.scalar.activation(out=inverse_squares[u][:], in_=inverses[u][:], func=ACT.Square)

        def coefficients(u):
            if in_range(u):
                half, s = divmod(u, S)
                grad_view = (
                    grad_turned[u // 2][:]
                    .rearrange("i j b -> i (j b)")
                    .bitcast(BF16)
                    .rearrange("i (j b e) -> i e b j", j=PACK, e=2)
                )
                grad_over_np = mid_tile("grad_over_np")
                nc.vector.tensor_tensor(out=grad_over_np[:], in0=grad_view[:, s % 2], in1=inverses[u][:], op=ALU.mult)
                ratios[u] = mid_tile("ratio")
                nc.vector.scalar_tensor_tensor(
                    out=ratios[u][:],
                    in0=by_token(dot_turned[u]),
                    scalar=-1.0,
                    in1=inverse_squares[u][:],
                    op0=ALU.mult,
                    op1=ALU.mult,
                )
                ca_f32[u] = mid_tile("ca_f32")
                nc.vector.tensor_tensor(
                    out=ca_f32[u][:], in0=grad_over_np[:], in1=by_token(inv_norm_q_turned[half]), op=ALU.mult
                )

        def round_ca(u):
            if in_range(u):
                grouped[u] = packed.tile([P, 2, P, PACK], BF16, name="grouped", tag="grouped", align_bytes=64)
                nc.scalar.copy(out=grouped[u][:, 0], in_=ca_f32[u][:])

        def compute_cb(u):
            if in_range(u):
                nc.gpsimd.tensor_tensor(out=grouped[u][:, 1], in0=ca_f32[u][:], in1=ratios[u][:], op=ALU.mult)

        def quantise(u):
            if in_range(u):
                codes[u] = packed.tile([P, 2 * P], U32, name="codes", tag="codes", align_bytes=64)
                scales[u] = packed.tile([P, 2 * P], U8, name="scales", tag="scales", align_bytes=64)
                nc.vector.quantize_mx(
                    out=codes[u][:].bitcast(E5M2_X4),
                    scales=scales[u][:],
                    in_=grouped[u][:].rearrange("i c b j -> i (c b j)"),
                )

        def d_columns(d_half):
            return slice(d_half * N_COLS, (d_half + 1) * N_COLS)

        def multiply_mx(u, d_half):
            if in_range(u):
                m1 = product_pool.tile([P, N_COLS], F32, name="m1", tag="m1")
                m2 = product_pool.tile([P, N_COLS], F32, name="m2", tag="m2")
                for which, product in enumerate((m1, m2)):
                    tokens = slice(which * P, (which + 1) * P)
                    nc.tensor.matmul_mx(
                        out=product[:],
                        lhsT=codes[u][:, tokens].bitcast(E5M2_X4),
                        lhsT_scale=scales[u][:, tokens],
                        rhs=w2_codes[:, d_columns(d_half)].bitcast(E4M3_X4),
                        rhs_scale=w2_scales[:, d_columns(d_half)],
                        start=True,
                        stop=True,
                    )
                products[(u, d_half)] = (m1, m2)

        def weigh(u, d_half):
            if in_range(u):
                if d_half == 0:
                    q_terms[u] = terms.tile([P, D], F32, name="q_term", tag="q_term")
                    p_terms[u] = terms.tile([P, D], F32, name="p_term", tag="p_term")
                cols = d_columns(d_half)
                m1, m2 = products[(u, d_half)]
                nc.vector.tensor_tensor(out=q_terms[u][:, cols], in0=m1[:], in1=q_last[u // S][:, cols], op=ALU.mult)
                nc.vector.tensor_tensor(out=p_terms[u][:, cols], in0=m2[:], in1=p_tiles[u][:, cols], op=ALU.mult)
                if d_half == D_HALVES - 1:
                    load_p(u + P_AHEAD)

        def add_terms(u, first_d_half, d_halves, adder):
            if in_range(u):
                half, s = divmod(u, S)
                cols = slice(first_d_half * N_COLS, (first_d_half + d_halves) * N_COLS)
                adder.tensor_tensor(out=q_terms[u][:, cols], in0=q_terms[u][:, cols], in1=p_terms[u][:, cols], op=ALU.add)
                nc.sync.dma_start(out=out[batch_rows(half), s, cols], in_=q_terms[u][:, cols])

        invert_norm_q(0)
        turn_inv_norm_q(0)


        for piece in range(4):
            d_cols = slice(piece * (D // 4), (piece + 1) * (D // 4))
            nc.scalar.activation(
                out=w2_grouped[:, d_cols, :],
                in_=w_rows[:, :, d_cols].rearrange("i j d -> i d j"),
                func=ACT.Square,
            )
            if piece % 2 == 1:
                d_half = slice((piece // 2) * N_COLS, (piece // 2 + 1) * N_COLS)
                nc.vector.quantize_mx(
                    out=w2_codes[:, d_half].bitcast(E4M3_X4),
                    scales=w2_scales[:, d_half],
                    in_=w2_grouped[:, d_half, :].rearrange("i d j -> i (d j)"),
                )


        last = UNITS - 1
        for t in range(-1, UNITS + OUT_LAG):
            residual(t)
            turn_norm_p(t + 1)
            correction(t)
            if t - OUT_LAG - 1 != last:
                add_terms(t - OUT_LAG - 1, 0, D_HALVES, nc.gpsimd)
            weigh(t - OUT_LAG, 0)
            inverse(t)
            guess(t + 1)
            coefficients(t - 1)
            if t - 1 == S - 1:
                turn_inv_norm_q(1)
            if t == 1:
                invert_norm_q(1)
            square_inverse(t)
            if t - OUT_LAG == last:
                add_terms(last, 0, 1, nc.gpsimd)
            turn_grad(t)
            turn_dot(t)
            quantise(t - MX_LAG)
            multiply_mx(t - MX_LAG, 0)
            round_ca(t - 1)
            compute_cb(t - 1)
            weigh(t - OUT_LAG, 1)
            multiply_mx(t - MX_LAG, 1)
            if t - OUT_LAG == last:
                add_terms(last, 1, 1, nc.vector)
